import numpy as np
import ml_dtypes


def mxq(x, axis, fmt="e4m3"):
    dtype, down = {"e4m3": (ml_dtypes.float8_e4m3fn, 7), "e5m2": (ml_dtypes.float8_e5m2, 14)}[fmt]
    v = np.moveaxis(np.asarray(x, np.float32).astype(ml_dtypes.bfloat16).astype(np.float64), axis, -1)
    blocks = v.reshape(v.shape[:-1] + (-1, 32))
    amax = np.abs(blocks).max(-1, keepdims=True)
    byte = np.maximum(np.where(amax > 0, np.frexp(amax)[1] - 1 + 127, 0) - down, 1)
    scale = np.exp2(byte - 127.0)
    codes = (blocks / scale).astype(np.float32).astype(dtype).astype(np.float64)
    return np.moveaxis((codes * scale).reshape(v.shape), -1, axis)


WIDE = False


def mx_kscale(k):
    if not WIDE:
        return np.ones(k)
    levels = np.array([10, -10, 5, -5, 0])
    a = np.random.permutation(np.resize(levels, k // 512 * 4)).reshape(k // 512, 4)
    idx = np.arange(k)
    return np.exp2(a[idx // 512, idx % 128 // 32])


BF16 = ml_dtypes.bfloat16


def bf(x):
    return np.asarray(x, np.float32).astype(BF16)


def f64(x):
    return np.asarray(x).astype(np.float64)


B, IN, E1, E2, LAT, D1, D2 = 128, 1024, 1536, 1024, 256, 512, 512


def silu(v):
    return v / (1.0 + np.exp(-v))


def softplus(v):
    return np.maximum(v, 0.0) + np.log(1.0 + np.exp(-np.abs(v)))


def sigmoid(v):
    return 1.0 / (1.0 + np.exp(-v))


def setup_inputs():
    s = mx_kscale(D1)
    return {
        'h_dec0': bf(silu(np.random.standard_normal((B, D1)) * 1.3) * s),
        'x': bf(np.random.uniform(0.0, 1.0, (B, IN))),
        'dw1': bf(np.random.standard_normal((D1, D2)) * 1.3 / np.sqrt(D1) / s[:, None]),
        'db1': bf(np.random.standard_normal(D2) * 0.3),
        'dw2': bf(np.random.standard_normal((D2, IN)) * 1.6 / np.sqrt(D2)),
        'db2': bf(np.random.standard_normal(IN) * 0.3 - 0.5),
    }


def reference(h_dec0, x, dw1, db1, dw2, db2):
    h = silu((mxq(f64(h_dec0), 1, 'e4m3') @ mxq(f64(dw1), 0, 'e4m3')) + f64(db1))
    logits = (mxq(h, 1, 'e4m3') @ mxq(f64(dw2), 0, 'e4m3')) + f64(db2)
    bce = np.maximum(logits, 0.0) - logits * f64(x) + softplus(-np.abs(logits))
    return bce.sum(-1), sigmoid(logits)

@@ -1,0 +1,198 @@
+import concourse.mybir as mybir
+from concourse.masks import make_identity
+
+FP8X4 = mybir.dt.float8_e4m3fn_x4
+BF16 = mybir.dt.bfloat16
+F32 = mybir.dt.float32
+U32 = mybir.dt.uint32
+U8 = mybir.dt.uint8
+ALU = mybir.AluOpType
+ACT = mybir.ActivationFunctionType
+AXIS = mybir.AxisListType
+
+P = 128
+PACK = 4
+BATCH = 128
+D1 = 512
+D2 = 512
+OUT = 1024
+BLOCK = 512
+SHARE = BLOCK // 2
+RUN = 4
+
+FLOPS = 2 * BATCH * D1 * D2 + 2 * BATCH * D2 * OUT
+
+
+def load_block(nc, raw, weight, cols):
+    nc.sync.dma_start(
+        out=raw[:, :, cols], in_=weight[:, cols].rearrange("(t p) c -> p t c", p=P)
+    )
+
+
+def regroup(copy, grouped, raw, cols):
+    copy(
+        out=grouped[:, cols, :].rearrange("p (c i) t -> p c t i", i=RUN),
+        in_=raw[:, :, cols].rearrange("p t (c i) -> p c t i", i=RUN),
+    )
+
+
+def quantise(nc, codes, scales, grouped, cols):
+    nc.vector.quantize_mx(
+        out=codes[:, cols].bitcast(FP8X4),
+        scales=scales[:, cols],
+        in_=grouped[:, cols, :].rearrange("p c t -> p (c t)"),
+    )
+
+
+def prepare_block(nc, codes, scales, grouped, raw, first):
+    vector_cols = slice(first, first + SHARE)
+    scalar_cols = slice(first + SHARE, first + BLOCK)
+    regroup(nc.vector.tensor_copy, grouped, raw, vector_cols)
+    regroup(nc.scalar.copy, grouped, raw, scalar_cols)
+    quantise(nc, codes, scales, grouped, vector_cols)
+    quantise(nc, codes, scales, grouped, scalar_cols)
+
+
+def tile_vae_pb_s_kernel(tc, h_dec0, x, dw1, db1, dw2, db2, out_0, out_1):
+    nc = tc.nc
+    with tc.tile_pool(name="sbuf", bufs=1) as sbuf, tc.psum_pool(name="psum", bufs=1) as psum:
+        ident_bf = sbuf.tile([P, P], BF16)
+        make_identity(nc, ident_bf[:])
+        ident_f32 = sbuf.tile([P, P], F32)
+        make_identity(nc, ident_f32[:])
+        half = sbuf.tile([P, 1], F32)
+        nc.vector.memset(half[:], 0.5)
+        warm = sbuf.tile([P, 1], F32)
+        nc.scalar.activation(out=warm[:], in_=half[:], func=ACT.Silu)
+
+        bias_rows = sbuf.tile([P, P], BF16)
+        nc.vector.memset(bias_rows[:], 0.0)
+        nc.scalar.dma_start(out=bias_rows[0:8, :], in_=db2.rearrange("(c n) -> c n", n=P))
+        nc.scalar.dma_start(out=bias_rows[8:12, :], in_=db1.rearrange("(c n) -> c n", n=P))
+        a_rows = sbuf.tile([BATCH, D1], BF16)
+        nc.scalar.dma_start(out=a_rows[:], in_=h_dec0)
+        raw1 = sbuf.tile([P, PACK, D2], BF16)
+        raw2 = sbuf.tile([P, PACK, OUT], BF16)
+        load_block(nc, raw1, dw1, slice(0, BLOCK))
+        load_block(nc, raw2, dw2, slice(0, BLOCK))
+        load_block(nc, raw2, dw2, slice(BLOCK, 2 * BLOCK))
+        x_sb = sbuf.tile([BATCH, OUT], BF16)
+        nc.sync.dma_start(out=x_sb[:], in_=x)
+
+        bias_t_ps = psum.tile([P, P], BF16)
+        nc.tensor.transpose(bias_t_ps[:], bias_rows[:], ident_bf[:])
+        bias_cols = sbuf.tile([P, 12], BF16)
+        nc.scalar.copy(out=bias_cols[:], in_=bias_t_ps[:, 0:12])
+        db2_ps = psum.tile([P, OUT], BF16)
+        for c in range(OUT // P):
+            nc.tensor.transpose(
+                db2_ps[:, c * P : (c + 1) * P],
+                bias_cols[:, c : c + 1].to_broadcast([P, P]),
+                ident_bf[:],
+            )
+        db2_all = sbuf.tile([P, OUT], BF16)
+        nc.scalar.copy(out=db2_all[:], in_=db2_ps[:])
+
+        a_t_ps = psum.tile([P, PACK, BATCH], BF16)
+        for t in range(PACK):
+            nc.tensor.transpose(a_t_ps[:, t, :], a_rows[:, t * P : (t + 1) * P], ident_bf[:])
+        a_grouped = sbuf.tile([P, BATCH, PACK], BF16, align_bytes=64)
+        nc.scalar.copy(out=a_grouped[:], in_=a_t_ps[:].rearrange("p t b -> p b t"))
+        a_codes = sbuf.tile([P, BATCH], U32, align_bytes=64)
+        a_scales = sbuf.tile([P, BATCH], U8, align_bytes=64)
+        quantise(nc, a_codes, a_scales, a_grouped, slice(0, BATCH))
+
+        grouped1 = sbuf.tile([P, D2, PACK], BF16, align_bytes=64)
+        codes1 = sbuf.tile([P, D2], U32, align_bytes=64)
+        scales1 = sbuf.tile([P, D2], U8, align_bytes=64)
+        prepare_block(nc, codes1, scales1, grouped1, raw1, 0)
+
+        h_ps = psum.tile([P, PACK, BATCH], F32)
+        for t in range(PACK):
+            cols = slice(t * P, (t + 1) * P)
+            nc.tensor.matmul_mx(
+                out=h_ps[:, t, :],
+                lhsT=codes1[:, cols].bitcast(FP8X4),
+                lhsT_scale=scales1[:, cols],
+                rhs=a_codes[:].bitcast(FP8X4),
+                rhs_scale=a_scales[:],
+                start=True,
+                stop=True,
+            )
+        pre = sbuf.tile([P, BATCH, PACK], F32)
+        nc.vector.tensor_tensor(
+            out=pre[:],
+            in0=h_ps[:].rearrange("p t b -> p b t"),
+            in1=bias_cols[:, 8:12].unsqueeze(1).to_broadcast([P, BATCH, PACK]),
+            op=ALU.add,
+        )
+        h_grouped = sbuf.tile([P, BATCH, PACK], BF16, align_bytes=64)
+        nc.scalar.activation(out=h_grouped[:], in_=pre[:], func=ACT.Silu)
+        h_codes = sbuf.tile([P, BATCH], U32, align_bytes=64)
+        h_scales = sbuf.tile([P, BATCH], U8, align_bytes=64)
+        quantise(nc, h_codes, h_scales, h_grouped, slice(0, BATCH))
+
+        grouped2 = sbuf.tile([P, OUT, PACK], BF16, align_bytes=64)
+        codes2 = sbuf.tile([P, OUT], U32, align_bytes=64)
+        scales2 = sbuf.tile([P, OUT], U8, align_bytes=64)
+        for first in range(0, OUT, BLOCK):
+            prepare_block(nc, codes2, scales2, grouped2, raw2, first)
+
+        z = sbuf.tile([BATCH, OUT], F32)
+        th = sbuf.tile([BATCH, OUT], F32)
+        sig = sbuf.tile([BATCH, OUT], F32)
+        abs_th = sbuf.tile([BATCH, OUT], F32)
+        relu_z = sbuf.tile([BATCH, OUT], F32)
+        minus_zx = sbuf.tile([BATCH, OUT], F32)
+        log_part = sbuf.tile([BATCH, OUT], F32)
+        vector_sums = sbuf.tile([BATCH, 4], F32)
+        scalar_sums = sbuf.tile([BATCH, 2], F32)
+        for b in range(OUT // BLOCK):
+            cols = slice(b * BLOCK, (b + 1) * BLOCK)
+            logits_ps = psum.tile([BATCH, BLOCK], F32, name="logits_ps%d" % b)
+            nc.tensor.matmul_mx(
+                out=logits_ps[:],
+                lhsT=h_codes[:].bitcast(FP8X4),
+                lhsT_scale=h_scales[:],
+                rhs=codes2[:, cols].bitcast(FP8X4),
+                rhs_scale=scales2[:, cols],
+                start=True,
+                stop=True,
+            )
+            nc.vector.tensor_tensor(out=z[:, cols], in0=logits_ps[:], in1=db2_all[:, cols], op=ALU.add)
+            nc.scalar.activation(out=th[:, cols], in_=z[:, cols], func=ACT.Tanh, scale=0.5)
+            nc.vector.tensor_scalar(
+                out=sig[:, cols], in0=th[:, cols], scalar1=0.5, scalar2=0.5, op0=ALU.mult, op1=ALU.add
+            )
+            nc.sync.dma_start(out=out_1[:, cols], in_=sig[:, cols])
+            nc.vector.scalar_tensor_tensor(
+                out=abs_th[:, cols], in0=th[:, cols], scalar=-1.0, in1=th[:, cols],
+                op0=ALU.mult, op1=ALU.max,
+            )
+            nc.vector.tensor_scalar(
+                out=relu_z[:, cols], in0=z[:, cols], scalar1=0.0, scalar2=None,
+                op0=ALU.max, op1=ALU.add, accum_out=vector_sums[:, b : b + 1],
+            )
+            nc.vector.scalar_tensor_tensor(
+                out=minus_zx[:, cols], in0=z[:, cols], scalar=-1.0, in1=x_sb[:, cols],
+                op0=ALU.mult, op1=ALU.mult, accum_out=vector_sums[:, 2 + b : 3 + b],
+            )
+        for b in range(OUT // BLOCK):
+            cols = slice(b * BLOCK, (b + 1) * BLOCK)
+            nc.scalar.activation(
+                out=log_part[:, cols], in_=abs_th[:, cols], func=ACT.Ln, scale=0.5, bias=half[:],
+                accum_out=scalar_sums[:, b : b + 1],
+            )
+
+        vector_total = sbuf.tile([BATCH, 1], F32)
+        nc.vector.tensor_reduce(out=vector_total[:], in_=vector_sums[:], axis=AXIS.X, op=ALU.add)
+        bce_col = sbuf.tile([BATCH, 1], F32)
+        nc.vector.tensor_scalar(
+            out=bce_col[:], in0=vector_total[:], scalar1=scalar_sums[:, 0:1], scalar2=scalar_sums[:, 1:2],
+            op0=ALU.subtract, op1=ALU.subtract,
+        )
+        bce_ps = psum.tile([P, BATCH], F32)
+        nc.tensor.transpose(bce_ps[:], bce_col[:, 0:1].to_broadcast([BATCH, P]), ident_f32[:])
+        bce_rows = sbuf.tile([P, BATCH], F32)
+        nc.vector.tensor_copy(out=bce_rows[:], in_=bce_ps[:])
+        nc.sync.dma_start(out=out_0.rearrange("(o b) -> o b", o=1), in_=bce_rows[0:1, :])

@@ -19,24 +19,28 @@ OUT = 1024
 BLOCK = 512
 SHARE = BLOCK // 2
 RUN = 4
+DB2_ROWS = OUT // P
 
 FLOPS = 2 * BATCH * D1 * D2 + 2 * BATCH * D2 * OUT
 
 
-def load_block(nc, raw, weight, cols):
+def load_block(nc, raw, weight, first):
+    cols = slice(first, first + BLOCK)
     nc.sync.dma_start(
         out=raw[:, :, cols], in_=weight[:, cols].rearrange("(t p) c -> p t c", p=P)
     )
 
 
-def regroup(copy, grouped, raw, cols):
+def regroup(copy, grouped, raw, first):
+    cols = slice(first, first + SHARE)
     copy(
         out=grouped[:, cols, :].rearrange("p (c i) t -> p c t i", i=RUN),
         in_=raw[:, :, cols].rearrange("p t (c i) -> p c t i", i=RUN),
     )
 
 
-def quantise(nc, codes, scales, grouped, cols):
+def quantise(nc, codes, scales, grouped, first, width):
+    cols = slice(first, first + width)
     nc.vector.quantize_mx(
         out=codes[:, cols].bitcast(FP8X4),
         scales=scales[:, cols],
@@ -44,18 +48,29 @@ def quantise(nc, codes, scales, grouped, cols):
     )
 
 
-def prepare_block(nc, codes, scales, grouped, raw, first):
-    vector_cols = slice(first, first + SHARE)
-    scalar_cols = slice(first + SHARE, first + BLOCK)
-    regroup(nc.vector.tensor_copy, grouped, raw, vector_cols)
-    regroup(nc.scalar.copy, grouped, raw, scalar_cols)
-    quantise(nc, codes, scales, grouped, vector_cols)
-    quantise(nc, codes, scales, grouped, scalar_cols)
-
-
 def tile_vae_pb_s_kernel(tc, h_dec0, x, dw1, db1, dw2, db2, out_0, out_1):
     nc = tc.nc
-    with tc.tile_pool(name="sbuf", bufs=1) as sbuf, tc.psum_pool(name="psum", bufs=1) as psum:
+    with tc.tile_pool(name="sbuf", bufs=1) as sbuf, tc.psum_pool(
+        name="psum", bufs=1
+    ) as psum, tc.manual_schedule():
+        bias_rows = sbuf.tile([P, P], BF16)
+        nc.vector.memset(bias_rows[:], 0.0)
+        nc.scalar.dma_start(
+            out=bias_rows[0:DB2_ROWS, :], in_=db2.rearrange("(c n) -> c n", n=P)
+        )
+        nc.scalar.dma_start(
+            out=bias_rows[DB2_ROWS : DB2_ROWS + PACK, :], in_=db1.rearrange("(c n) -> c n", n=P)
+        )
+        a_rows = sbuf.tile([BATCH, D1], BF16)
+        nc.sync.dma_start(out=a_rows[:], in_=h_dec0)
+        raw1 = sbuf.tile([P, PACK, D2], BF16)
+        raw2 = sbuf.tile([P, PACK, OUT], BF16)
+        load_block(nc, raw1, dw1, 0)
+        load_block(nc, raw2, dw2, 0)
+        load_block(nc, raw2, dw2, BLOCK)
+        x_sb = sbuf.tile([BATCH, OUT], BF16)
+        nc.sync.dma_start(out=x_sb[:], in_=x)
+
         ident_bf = sbuf.tile([P, P], BF16)
         make_identity(nc, ident_bf[:])
         ident_f32 = sbuf.tile([P, P], F32)
@@ -65,33 +80,10 @@ def tile_vae_pb_s_kernel(tc, h_dec0, x, dw1, db1, dw2, db2, out_0, out_1):
         warm = sbuf.tile([P, 1], F32)
         nc.scalar.activation(out=warm[:], in_=half[:], func=ACT.Silu)
 
-        bias_rows = sbuf.tile([P, P], BF16)
-        nc.vector.memset(bias_rows[:], 0.0)
-        nc.scalar.dma_start(out=bias_rows[0:8, :], in_=db2.rearrange("(c n) -> c n", n=P))
-        nc.scalar.dma_start(out=bias_rows[8:12, :], in_=db1.rearrange("(c n) -> c n", n=P))
-        a_rows = sbuf.tile([BATCH, D1], BF16)
-        nc.scalar.dma_start(out=a_rows[:], in_=h_dec0)
-        raw1 = sbuf.tile([P, PACK, D2], BF16)
-        raw2 = sbuf.tile([P, PACK, OUT], BF16)
-        load_block(nc, raw1, dw1, slice(0, BLOCK))
-        load_block(nc, raw2, dw2, slice(0, BLOCK))
-        load_block(nc, raw2, dw2, slice(BLOCK, 2 * BLOCK))
-        x_sb = sbuf.tile([BATCH, OUT], BF16)
-        nc.sync.dma_start(out=x_sb[:], in_=x)
-
         bias_t_ps = psum.tile([P, P], BF16)
         nc.tensor.transpose(bias_t_ps[:], bias_rows[:], ident_bf[:])
-        bias_cols = sbuf.tile([P, 12], BF16)
-        nc.scalar.copy(out=bias_cols[:], in_=bias_t_ps[:, 0:12])
-        db2_ps = psum.tile([P, OUT], BF16)
-        for c in range(OUT // P):
-            nc.tensor.transpose(
-                db2_ps[:, c * P : (c + 1) * P],
-                bias_cols[:, c : c + 1].to_broadcast([P, P]),
-                ident_bf[:],
-            )
-        db2_all = sbuf.tile([P, OUT], BF16)
-        nc.scalar.copy(out=db2_all[:], in_=db2_ps[:])
+        bias_cols = sbuf.tile([P, DB2_ROWS + PACK], BF16)
+        nc.scalar.copy(out=bias_cols[:], in_=bias_t_ps[:, 0 : DB2_ROWS + PACK])
 
         a_t_ps = psum.tile([P, PACK, BATCH], BF16)
         for t in range(PACK):
@@ -100,14 +92,26 @@ def tile_vae_pb_s_kernel(tc, h_dec0, x, dw1, db1, dw2, db2, out_0, out_1):
         nc.scalar.copy(out=a_grouped[:], in_=a_t_ps[:].rearrange("p t b -> p b t"))
         a_codes = sbuf.tile([P, BATCH], U32, align_bytes=64)
         a_scales = sbuf.tile([P, BATCH], U8, align_bytes=64)
-        quantise(nc, a_codes, a_scales, a_grouped, slice(0, BATCH))
+        quantise(nc, a_codes, a_scales, a_grouped, 0, BATCH)
+
+        db2_ps = psum.tile([P, OUT], BF16)
+        for c in range(DB2_ROWS):
+            nc.tensor.transpose(
+                db2_ps[:, c * P : (c + 1) * P],
+                bias_cols[:, c : c + 1].to_broadcast([P, P]),
+                ident_bf[:],
+            )
 
         grouped1 = sbuf.tile([P, D2, PACK], BF16, align_bytes=64)
         codes1 = sbuf.tile([P, D2], U32, align_bytes=64)
         scales1 = sbuf.tile([P, D2], U8, align_bytes=64)
-        prepare_block(nc, codes1, scales1, grouped1, raw1, 0)
+        regroup(nc.vector.tensor_copy, grouped1, raw1, 0)
+        regroup(nc.scalar.copy, grouped1, raw1, SHARE)
+        quantise(nc, codes1, scales1, grouped1, 0, SHARE)
+        quantise(nc, codes1, scales1, grouped1, SHARE, SHARE)
 
         h_ps = psum.tile([P, PACK, BATCH], F32)
+        h_planes = sbuf.tile([P, PACK, BATCH], BF16)
         for t in range(PACK):
             cols = slice(t * P, (t + 1) * P)
             nc.tensor.matmul_mx(
@@ -119,34 +123,32 @@ def tile_vae_pb_s_kernel(tc, h_dec0, x, dw1, db1, dw2, db2, out_0, out_1):
                 start=True,
                 stop=True,
             )
-        pre = sbuf.tile([P, BATCH, PACK], F32)
-        nc.vector.tensor_tensor(
-            out=pre[:],
-            in0=h_ps[:].rearrange("p t b -> p b t"),
-            in1=bias_cols[:, 8:12].unsqueeze(1).to_broadcast([P, BATCH, PACK]),
-            op=ALU.add,
-        )
-        h_grouped = sbuf.tile([P, BATCH, PACK], BF16, align_bytes=64)
-        nc.scalar.activation(out=h_grouped[:], in_=pre[:], func=ACT.Silu)
-        h_codes = sbuf.tile([P, BATCH], U32, align_bytes=64)
-        h_scales = sbuf.tile([P, BATCH], U8, align_bytes=64)
-        quantise(nc, h_codes, h_scales, h_grouped, slice(0, BATCH))
+            nc.scalar.activation(
+                out=h_planes[:, t, :], in_=h_ps[:, t, :], func=ACT.Silu,
+                bias=bias_cols[:, DB2_ROWS + t : DB2_ROWS + t + 1],
+            )
 
         grouped2 = sbuf.tile([P, OUT, PACK], BF16, align_bytes=64)
         codes2 = sbuf.tile([P, OUT], U32, align_bytes=64)
         scales2 = sbuf.tile([P, OUT], U8, align_bytes=64)
-        for first in range(0, OUT, BLOCK):
-            prepare_block(nc, codes2, scales2, grouped2, raw2, first)
+        h_grouped = sbuf.tile([P, BATCH, PACK], BF16, align_bytes=64)
+        h_codes = sbuf.tile([P, BATCH], U32, align_bytes=64)
+        h_scales = sbuf.tile([P, BATCH], U8, align_bytes=64)
+        regroup(nc.vector.tensor_copy, grouped2, raw2, 0)
+        regroup(nc.scalar.copy, grouped2, raw2, SHARE)
+        nc.vector.tensor_copy(out=h_grouped[:], in_=h_planes[:].rearrange("p t b -> p b t"))
+        quantise(nc, codes2, scales2, grouped2, 0, SHARE)
+        quantise(nc, h_codes, h_scales, h_grouped, 0, BATCH)
+        regroup(nc.vector.tensor_copy, grouped2, raw2, BLOCK)
+        regroup(nc.scalar.copy, grouped2, raw2, BLOCK + SHARE)
+        quantise(nc, codes2, scales2, grouped2, SHARE, SHARE)
+        quantise(nc, codes2, scales2, grouped2, BLOCK, SHARE)
+        quantise(nc, codes2, scales2, grouped2, BLOCK + SHARE, SHARE)
+        db2_all = sbuf.tile([P, OUT], BF16)
+        nc.scalar.copy(out=db2_all[:], in_=db2_ps[:])
 
         z = sbuf.tile([BATCH, OUT], F32)
         th = sbuf.tile([BATCH, OUT], F32)
-        sig = sbuf.tile([BATCH, OUT], F32)
-        abs_th = sbuf.tile([BATCH, OUT], F32)
-        relu_z = sbuf.tile([BATCH, OUT], F32)
-        minus_zx = sbuf.tile([BATCH, OUT], F32)
-        log_part = sbuf.tile([BATCH, OUT], F32)
-        vector_sums = sbuf.tile([BATCH, 4], F32)
-        scalar_sums = sbuf.tile([BATCH, 2], F32)
         for b in range(OUT // BLOCK):
             cols = slice(b * BLOCK, (b + 1) * BLOCK)
             logits_ps = psum.tile([BATCH, BLOCK], F32, name="logits_ps%d" % b)
@@ -159,38 +161,46 @@ def tile_vae_pb_s_kernel(tc, h_dec0, x, dw1, db1, dw2, db2, out_0, out_1):
                 start=True,
                 stop=True,
             )
-            nc.vector.tensor_tensor(out=z[:, cols], in0=logits_ps[:], in1=db2_all[:, cols], op=ALU.add)
+            nc.vector.tensor_tensor(
+                out=z[:, cols], in0=logits_ps[:], in1=db2_all[:, cols], op=ALU.add
+            )
             nc.scalar.activation(out=th[:, cols], in_=z[:, cols], func=ACT.Tanh, scale=0.5)
+
+        sig = sbuf.tile([BATCH, OUT], F32)
+        abs_th = sbuf.tile([BATCH, OUT], F32)
+        relu_z = sbuf.tile([BATCH, OUT], F32)
+        minus_zx = sbuf.tile([BATCH, OUT], F32)
+        log_part = sbuf.tile([BATCH, OUT], F32)
+        vector_sums = sbuf.tile([BATCH, 3], F32)
+        log_sum = sbuf.tile([BATCH, 1], F32)
+        for b in range(OUT // BLOCK):
+            cols = slice(b * BLOCK, (b + 1) * BLOCK)
             nc.vector.tensor_scalar(
-                out=sig[:, cols], in0=th[:, cols], scalar1=0.5, scalar2=0.5, op0=ALU.mult, op1=ALU.add
+                out=sig[:, cols], in0=th[:, cols], scalar1=0.5, scalar2=0.5,
+                op0=ALU.mult, op1=ALU.add,
             )
             nc.sync.dma_start(out=out_1[:, cols], in_=sig[:, cols])
-            nc.vector.scalar_tensor_tensor(
-                out=abs_th[:, cols], in0=th[:, cols], scalar=-1.0, in1=th[:, cols],
-                op0=ALU.mult, op1=ALU.max,
-            )
             nc.vector.tensor_scalar(
                 out=relu_z[:, cols], in0=z[:, cols], scalar1=0.0, scalar2=None,
                 op0=ALU.max, op1=ALU.add, accum_out=vector_sums[:, b : b + 1],
             )
-            nc.vector.scalar_tensor_tensor(
-                out=minus_zx[:, cols], in0=z[:, cols], scalar=-1.0, in1=x_sb[:, cols],
-                op0=ALU.mult, op1=ALU.mult, accum_out=vector_sums[:, 2 + b : 3 + b],
-            )
-        for b in range(OUT // BLOCK):
-            cols = slice(b * BLOCK, (b + 1) * BLOCK)
-            nc.scalar.activation(
-                out=log_part[:, cols], in_=abs_th[:, cols], func=ACT.Ln, scale=0.5, bias=half[:],
-                accum_out=scalar_sums[:, b : b + 1],
-            )
+            if b == 0:
+                nc.vector.scalar_tensor_tensor(
+                    out=abs_th[:], in0=th[:], scalar=-1.0, in1=th[:], op0=ALU.mult, op1=ALU.max
+                )
+                nc.scalar.activation(
+                    out=log_part[:], in_=abs_th[:], func=ACT.Ln, scale=0.5, bias=half[:],
+                    accum_out=log_sum[:],
+                )
+        nc.vector.scalar_tensor_tensor(
+            out=minus_zx[:], in0=z[:], scalar=-1.0, in1=x_sb[:],
+            op0=ALU.mult, op1=ALU.mult, accum_out=vector_sums[:, 2:3],
+        )
 
         vector_total = sbuf.tile([BATCH, 1], F32)
         nc.vector.tensor_reduce(out=vector_total[:], in_=vector_sums[:], axis=AXIS.X, op=ALU.add)
         bce_col = sbuf.tile([BATCH, 1], F32)
-        nc.vector.tensor_scalar(
-            out=bce_col[:], in0=vector_total[:], scalar1=scalar_sums[:, 0:1], scalar2=scalar_sums[:, 1:2],
-            op0=ALU.subtract, op1=ALU.subtract,
-        )
+        nc.vector.tensor_tensor(out=bce_col[:], in0=vector_total[:], in1=log_sum[:], op=ALU.subtract)
         bce_ps = psum.tile([P, BATCH], F32)
         nc.tensor.transpose(bce_ps[:], bce_col[:, 0:1].to_broadcast([BATCH, P]), ident_f32[:])
         bce_rows = sbuf.tile([P, BATCH], F32)

@@ -8,10 +8,10 @@ U32 = mybir.dt.uint32
 U8 = mybir.dt.uint8
 ALU = mybir.AluOpType
 ACT = mybir.ActivationFunctionType
-AXIS = mybir.AxisListType
 
 P = 128
 PACK = 4
+PAIR = 2
 BATCH = 128
 D1 = 512
 D2 = 512
@@ -20,15 +20,9 @@ BLOCK = 512
 SHARE = BLOCK // 2
 RUN = 4
 DB2_ROWS = OUT // P
+SQUARE = 32
 
 FLOPS = 2 * BATCH * D1 * D2 + 2 * BATCH * D2 * OUT
-
-
-def load_block(nc, raw, weight, first):
-    cols = slice(first, first + BLOCK)
-    nc.sync.dma_start(
-        out=raw[:, :, cols], in_=weight[:, cols].rearrange("(t p) c -> p t c", p=P)
-    )
 
 
 def regroup(copy, grouped, raw, first):
@@ -39,12 +33,11 @@ def regroup(copy, grouped, raw, first):
     )
 
 
-def quantise(nc, codes, scales, grouped, first, width):
-    cols = slice(first, first + width)
+def quantise(nc, codes, scales, values, first, width):
     nc.vector.quantize_mx(
-        out=codes[:, cols].bitcast(FP8X4),
-        scales=scales[:, cols],
-        in_=grouped[:, cols, :].rearrange("p c t -> p (c t)"),
+        out=codes[:, first : first + width].bitcast(FP8X4),
+        scales=scales[:, first : first + width],
+        in_=values[:, PACK * first : PACK * (first + width)],
     )
 
 
@@ -53,46 +46,92 @@ def tile_vae_pb_s_kernel(tc, h_dec0, x, dw1, db1, dw2, db2, out_0, out_1):
     with tc.tile_pool(name="sbuf", bufs=1) as sbuf, tc.psum_pool(
         name="psum", bufs=1
     ) as psum, tc.manual_schedule():
-        bias_rows = sbuf.tile([P, P], BF16)
-        nc.vector.memset(bias_rows[:], 0.0)
-        nc.scalar.dma_start(
-            out=bias_rows[0:DB2_ROWS, :], in_=db2.rearrange("(c n) -> c n", n=P)
-        )
-        nc.scalar.dma_start(
-            out=bias_rows[DB2_ROWS : DB2_ROWS + PACK, :], in_=db1.rearrange("(c n) -> c n", n=P)
+        raw1 = sbuf.tile([P, PACK, D2], BF16)
+        nc.sync.dma_start(
+            out=raw1[:].rearrange("p (u e) c -> p u (e c)", e=PAIR),
+            in_=dw1.rearrange("(u p e) c -> p u (e c)", p=P, e=PAIR),
         )
         a_rows = sbuf.tile([BATCH, D1], BF16)
         nc.sync.dma_start(out=a_rows[:], in_=h_dec0)
-        raw1 = sbuf.tile([P, PACK, D2], BF16)
+        bias_rows = sbuf.tile([P, P], BF16)
+        nc.vector.memset(bias_rows[:], 0.0)
+        nc.sync.dma_start(out=bias_rows[0:DB2_ROWS, :], in_=db2.rearrange("(c n) -> c n", n=P))
+        nc.sync.dma_start(
+            out=bias_rows[DB2_ROWS : DB2_ROWS + PACK, :], in_=db1.rearrange("(c n) -> c n", n=P)
+        )
         raw2 = sbuf.tile([P, PACK, OUT], BF16)
-        load_block(nc, raw1, dw1, 0)
-        load_block(nc, raw2, dw2, 0)
-        load_block(nc, raw2, dw2, BLOCK)
+        for first in range(0, OUT, BLOCK):
+            cols = slice(first, first + BLOCK)
+            nc.sync.dma_start(
+                out=raw2[:, :, cols], in_=dw2[:, cols].rearrange("(t p) c -> p t c", p=P)
+            )
         x_sb = sbuf.tile([BATCH, OUT], BF16)
         nc.sync.dma_start(out=x_sb[:], in_=x)
 
-        ident_bf = sbuf.tile([P, P], BF16)
-        make_identity(nc, ident_bf[:])
         ident_f32 = sbuf.tile([P, P], F32)
         make_identity(nc, ident_f32[:])
+        ident_bf = sbuf.tile([P, P], BF16)
+        make_identity(nc, ident_bf[:])
         half = sbuf.tile([P, 1], F32)
         nc.vector.memset(half[:], 0.5)
+        bce_cols = sbuf.tile([BATCH, SQUARE], F32, align_bytes=64)
+        nc.vector.memset(bce_cols[:], 0.0)
         warm = sbuf.tile([P, 1], F32)
         nc.scalar.activation(out=warm[:], in_=half[:], func=ACT.Silu)
+
+        grouped1 = sbuf.tile([P, D2, PACK], BF16, align_bytes=64)
+        codes1 = sbuf.tile([P, D2], U32, align_bytes=64)
+        scales1 = sbuf.tile([P, D2], U8, align_bytes=64)
+        values1 = grouped1[:].rearrange("p c t -> p (c t)")
+        regroup(nc.vector.tensor_copy, grouped1, raw1, 0)
+        regroup(nc.scalar.copy, grouped1, raw1, SHARE)
+        quantise(nc, codes1, scales1, values1, 0, SHARE)
+        quantise(nc, codes1, scales1, values1, SHARE, SHARE)
+
+        a_words = a_rows[:].bitcast(F32)
+        a_t_ps = psum.tile([P, PAIR, BATCH], F32)
+        for u in range(PAIR):
+            nc.tensor.transpose(a_t_ps[:, u, :], a_words[:, u * P : (u + 1) * P], ident_f32[:])
+        a_grouped = sbuf.tile([P, BATCH, PAIR], F32, align_bytes=64)
+        nc.scalar.copy(out=a_grouped[:], in_=a_t_ps[:].rearrange("p u b -> p b u"))
+        a_codes = sbuf.tile([P, BATCH], U32, align_bytes=64)
+        a_scales = sbuf.tile([P, BATCH], U8, align_bytes=64)
+        quantise(
+            nc, a_codes, a_scales, a_grouped[:].rearrange("p b u -> p (b u)").bitcast(BF16), 0, BATCH
+        )
 
         bias_t_ps = psum.tile([P, P], BF16)
         nc.tensor.transpose(bias_t_ps[:], bias_rows[:], ident_bf[:])
         bias_cols = sbuf.tile([P, DB2_ROWS + PACK], BF16)
         nc.scalar.copy(out=bias_cols[:], in_=bias_t_ps[:, 0 : DB2_ROWS + PACK])
 
-        a_t_ps = psum.tile([P, PACK, BATCH], BF16)
+        grouped2 = sbuf.tile([P, OUT, PACK], BF16, align_bytes=64)
+        codes2 = sbuf.tile([P, OUT], U32, align_bytes=64)
+        scales2 = sbuf.tile([P, OUT], U8, align_bytes=64)
+        values2 = grouped2[:].rearrange("p c t -> p (c t)")
+        regroup(nc.scalar.copy, grouped2, raw2, SHARE)
+        h_ps = [psum.tile([P, PAIR, BATCH], F32, name="h_ps%d" % i) for i in range(PACK // PAIR)]
         for t in range(PACK):
-            nc.tensor.transpose(a_t_ps[:, t, :], a_rows[:, t * P : (t + 1) * P], ident_bf[:])
-        a_grouped = sbuf.tile([P, BATCH, PACK], BF16, align_bytes=64)
-        nc.scalar.copy(out=a_grouped[:], in_=a_t_ps[:].rearrange("p t b -> p b t"))
-        a_codes = sbuf.tile([P, BATCH], U32, align_bytes=64)
-        a_scales = sbuf.tile([P, BATCH], U8, align_bytes=64)
-        quantise(nc, a_codes, a_scales, a_grouped, 0, BATCH)
+            cols = slice(t * P, (t + 1) * P)
+            nc.tensor.matmul_mx(
+                out=h_ps[t // PAIR][:, t % PAIR, :],
+                lhsT=codes1[:, cols].bitcast(FP8X4),
+                lhsT_scale=scales1[:, cols],
+                rhs=a_codes[:].bitcast(FP8X4),
+                rhs_scale=a_scales[:],
+                start=True,
+                stop=True,
+            )
+        h_planes = sbuf.tile([P, PACK, BATCH], BF16)
+        for t in range(PACK):
+            nc.scalar.activation(
+                out=h_planes[:, t, :], in_=h_ps[t // PAIR][:, t % PAIR, :], func=ACT.Silu,
+                bias=bias_cols[:, DB2_ROWS + t : DB2_ROWS + t + 1],
+            )
+        h_grouped = sbuf.tile([P, BATCH, PACK], BF16, align_bytes=64)
+        nc.scalar.copy(out=h_grouped[:], in_=h_planes[:].rearrange("p t b -> p b t"))
+        h_codes = sbuf.tile([P, BATCH], U32, align_bytes=64)
+        h_scales = sbuf.tile([P, BATCH], U8, align_bytes=64)
 
         db2_ps = psum.tile([P, OUT], BF16)
         for c in range(DB2_ROWS):
@@ -101,56 +140,22 @@ def tile_vae_pb_s_kernel(tc, h_dec0, x, dw1, db1, dw2, db2, out_0, out_1):
                 bias_cols[:, c : c + 1].to_broadcast([P, P]),
                 ident_bf[:],
             )
-
-        grouped1 = sbuf.tile([P, D2, PACK], BF16, align_bytes=64)
-        codes1 = sbuf.tile([P, D2], U32, align_bytes=64)
-        scales1 = sbuf.tile([P, D2], U8, align_bytes=64)
-        regroup(nc.vector.tensor_copy, grouped1, raw1, 0)
-        regroup(nc.scalar.copy, grouped1, raw1, SHARE)
-        quantise(nc, codes1, scales1, grouped1, 0, SHARE)
-        quantise(nc, codes1, scales1, grouped1, SHARE, SHARE)
-
-        h_ps = psum.tile([P, PACK, BATCH], F32)
-        h_planes = sbuf.tile([P, PACK, BATCH], BF16)
-        for t in range(PACK):
-            cols = slice(t * P, (t + 1) * P)
-            nc.tensor.matmul_mx(
-                out=h_ps[:, t, :],
-                lhsT=codes1[:, cols].bitcast(FP8X4),
-                lhsT_scale=scales1[:, cols],
-                rhs=a_codes[:].bitcast(FP8X4),
-                rhs_scale=a_scales[:],
-                start=True,
-                stop=True,
-            )
-            nc.scalar.activation(
-                out=h_planes[:, t, :], in_=h_ps[:, t, :], func=ACT.Silu,
-                bias=bias_cols[:, DB2_ROWS + t : DB2_ROWS + t + 1],
-            )
-
-        grouped2 = sbuf.tile([P, OUT, PACK], BF16, align_bytes=64)
-        codes2 = sbuf.tile([P, OUT], U32, align_bytes=64)
-        scales2 = sbuf.tile([P, OUT], U8, align_bytes=64)
-        h_grouped = sbuf.tile([P, BATCH, PACK], BF16, align_bytes=64)
-        h_codes = sbuf.tile([P, BATCH], U32, align_bytes=64)
-        h_scales = sbuf.tile([P, BATCH], U8, align_bytes=64)
-        regroup(nc.vector.tensor_copy, grouped2, raw2, 0)
-        regroup(nc.scalar.copy, grouped2, raw2, SHARE)
-        nc.vector.tensor_copy(out=h_grouped[:], in_=h_planes[:].rearrange("p t b -> p b t"))
-        quantise(nc, codes2, scales2, grouped2, 0, SHARE)
-        quantise(nc, h_codes, h_scales, h_grouped, 0, BATCH)
-        regroup(nc.vector.tensor_copy, grouped2, raw2, BLOCK)
-        regroup(nc.scalar.copy, grouped2, raw2, BLOCK + SHARE)
-        quantise(nc, codes2, scales2, grouped2, SHARE, SHARE)
-        quantise(nc, codes2, scales2, grouped2, BLOCK, SHARE)
-        quantise(nc, codes2, scales2, grouped2, BLOCK + SHARE, SHARE)
         db2_all = sbuf.tile([P, OUT], BF16)
         nc.scalar.copy(out=db2_all[:], in_=db2_ps[:])
 
+        regroup(nc.vector.tensor_copy, grouped2, raw2, 0)
+        regroup(nc.vector.tensor_copy, grouped2, raw2, BLOCK)
+        quantise(nc, codes2, scales2, values2, 0, SHARE)
+        regroup(nc.vector.tensor_copy, grouped2, raw2, BLOCK + SHARE)
+        quantise(nc, codes2, scales2, values2, SHARE, SHARE)
+        quantise(nc, codes2, scales2, values2, BLOCK, SHARE)
+        quantise(nc, h_codes, h_scales, h_grouped[:].rearrange("p b t -> p (b t)"), 0, BATCH)
+        quantise(nc, codes2, scales2, values2, BLOCK + SHARE, SHARE)
+
+        halves = [slice(first, first + BLOCK) for first in range(0, OUT, BLOCK)]
         z = sbuf.tile([BATCH, OUT], F32)
         th = sbuf.tile([BATCH, OUT], F32)
-        for b in range(OUT // BLOCK):
-            cols = slice(b * BLOCK, (b + 1) * BLOCK)
+        for b, cols in enumerate(halves):
             logits_ps = psum.tile([BATCH, BLOCK], F32, name="logits_ps%d" % b)
             nc.tensor.matmul_mx(
                 out=logits_ps[:],
@@ -171,38 +176,45 @@ def tile_vae_pb_s_kernel(tc, h_dec0, x, dw1, db1, dw2, db2, out_0, out_1):
         relu_z = sbuf.tile([BATCH, OUT], F32)
         minus_zx = sbuf.tile([BATCH, OUT], F32)
         log_part = sbuf.tile([BATCH, OUT], F32)
-        vector_sums = sbuf.tile([BATCH, 3], F32)
+        relu_sum_0 = sbuf.tile([BATCH, 1], F32)
         log_sum = sbuf.tile([BATCH, 1], F32)
-        for b in range(OUT // BLOCK):
-            cols = slice(b * BLOCK, (b + 1) * BLOCK)
+        vector_sums = sbuf.tile([BATCH, 2], F32)
+        for cols in halves:
+            nc.vector.scalar_tensor_tensor(
+                out=abs_th[:, cols], in0=th[:, cols], scalar=-1.0, in1=th[:, cols],
+                op0=ALU.mult, op1=ALU.max,
+            )
             nc.vector.tensor_scalar(
                 out=sig[:, cols], in0=th[:, cols], scalar1=0.5, scalar2=0.5,
                 op0=ALU.mult, op1=ALU.add,
             )
             nc.sync.dma_start(out=out_1[:, cols], in_=sig[:, cols])
-            nc.vector.tensor_scalar(
-                out=relu_z[:, cols], in0=z[:, cols], scalar1=0.0, scalar2=None,
-                op0=ALU.max, op1=ALU.add, accum_out=vector_sums[:, b : b + 1],
-            )
-            if b == 0:
-                nc.vector.scalar_tensor_tensor(
-                    out=abs_th[:], in0=th[:], scalar=-1.0, in1=th[:], op0=ALU.mult, op1=ALU.max
-                )
-                nc.scalar.activation(
-                    out=log_part[:], in_=abs_th[:], func=ACT.Ln, scale=0.5, bias=half[:],
-                    accum_out=log_sum[:],
-                )
+        nc.scalar.activation(
+            out=relu_z[:, halves[0]], in_=z[:, halves[0]], func=ACT.Relu, accum_out=relu_sum_0[:]
+        )
+        nc.vector.tensor_scalar(
+            out=relu_z[:, halves[1]], in0=z[:, halves[1]], scalar1=0.0, scalar2=None,
+            op0=ALU.max, op1=ALU.add, accum_out=vector_sums[:, 0:1],
+        )
+        nc.scalar.activation(
+            out=log_part[:], in_=abs_th[:], func=ACT.Ln, scale=0.5, bias=half[:],
+            accum_out=log_sum[:],
+        )
         nc.vector.scalar_tensor_tensor(
             out=minus_zx[:], in0=z[:], scalar=-1.0, in1=x_sb[:],
-            op0=ALU.mult, op1=ALU.mult, accum_out=vector_sums[:, 2:3],
+            op0=ALU.mult, op1=ALU.mult, accum_out=vector_sums[:, 1:2],
         )
 
         vector_total = sbuf.tile([BATCH, 1], F32)
-        nc.vector.tensor_reduce(out=vector_total[:], in_=vector_sums[:], axis=AXIS.X, op=ALU.add)
-        bce_col = sbuf.tile([BATCH, 1], F32)
-        nc.vector.tensor_tensor(out=bce_col[:], in0=vector_total[:], in1=log_sum[:], op=ALU.subtract)
-        bce_ps = psum.tile([P, BATCH], F32)
-        nc.tensor.transpose(bce_ps[:], bce_col[:, 0:1].to_broadcast([BATCH, P]), ident_f32[:])
-        bce_rows = sbuf.tile([P, BATCH], F32)
-        nc.vector.tensor_copy(out=bce_rows[:], in_=bce_ps[:])
-        nc.sync.dma_start(out=out_0.rearrange("(o b) -> o b", o=1), in_=bce_rows[0:1, :])
+        nc.vector.tensor_tensor(
+            out=vector_total[:], in0=vector_sums[:, 0:1], in1=vector_sums[:, 1:2], op=ALU.add
+        )
+        nc.vector.scalar_tensor_tensor(
+            out=bce_cols[:, 0:1], in0=relu_sum_0[:], scalar=log_sum[:], in1=vector_total[:],
+            op0=ALU.subtract, op1=ALU.add,
+        )
+        bce_rows = sbuf.tile([BATCH, SQUARE], F32, align_bytes=64)
+        nc.vector.transpose(out=bce_rows[:], in_=bce_cols[:])
+        nc.sync.dma_start(
+            out=out_0.rearrange("(q j) -> q j", j=SQUARE), in_=bce_rows[0:BATCH:SQUARE, :]
+        )

@@ -1,3 +1,5 @@
+import math
+
 import concourse.mybir as mybir
 from concourse.masks import make_identity
 
@@ -21,6 +23,8 @@ SHARE = BLOCK // 2
 RUN = 4
 DB2_ROWS = OUT // P
 SQUARE = 32
+CLAMP = 30.0
+SIGMOID_FLOOR = 1.0 / (1.0 + math.exp(CLAMP))
 
 FLOPS = 2 * BATCH * D1 * D2 + 2 * BATCH * D2 * OUT
 
@@ -141,7 +145,8 @@ def tile_vae_pb_s_kernel(tc, h_dec0, x, dw1, db1, dw2, db2, out_0, out_1):
                 ident_bf[:],
             )
         db2_all = sbuf.tile([P, OUT], BF16)
-        nc.scalar.copy(out=db2_all[:], in_=db2_ps[:])
+        warm_sigmoid = sbuf.tile([P, 1], F32)
+        nc.scalar.activation(out=warm_sigmoid[:], in_=half[:], func=ACT.Sigmoid)
 
         regroup(nc.vector.tensor_copy, grouped2, raw2, 0)
         regroup(nc.vector.tensor_copy, grouped2, raw2, BLOCK)
@@ -149,12 +154,13 @@ def tile_vae_pb_s_kernel(tc, h_dec0, x, dw1, db1, dw2, db2, out_0, out_1):
         regroup(nc.vector.tensor_copy, grouped2, raw2, BLOCK + SHARE)
         quantise(nc, codes2, scales2, values2, SHARE, SHARE)
         quantise(nc, codes2, scales2, values2, BLOCK, SHARE)
-        quantise(nc, h_codes, h_scales, h_grouped[:].rearrange("p b t -> p (b t)"), 0, BATCH)
         quantise(nc, codes2, scales2, values2, BLOCK + SHARE, SHARE)
+        quantise(nc, h_codes, h_scales, h_grouped[:].rearrange("p b t -> p (b t)"), 0, BATCH)
+        nc.vector.tensor_copy(out=db2_all[:], in_=db2_ps[:])
 
         halves = [slice(first, first + BLOCK) for first in range(0, OUT, BLOCK)]
         z = sbuf.tile([BATCH, OUT], F32)
-        th = sbuf.tile([BATCH, OUT], F32)
+        sig = sbuf.tile([BATCH, OUT], F32)
         for b, cols in enumerate(halves):
             logits_ps = psum.tile([BATCH, BLOCK], F32, name="logits_ps%d" % b)
             nc.tensor.matmul_mx(
@@ -169,49 +175,31 @@ def tile_vae_pb_s_kernel(tc, h_dec0, x, dw1, db1, dw2, db2, out_0, out_1):
             nc.vector.tensor_tensor(
                 out=z[:, cols], in0=logits_ps[:], in1=db2_all[:, cols], op=ALU.add
             )
-            nc.scalar.activation(out=th[:, cols], in_=z[:, cols], func=ACT.Tanh, scale=0.5)
-
-        sig = sbuf.tile([BATCH, OUT], F32)
-        abs_th = sbuf.tile([BATCH, OUT], F32)
-        relu_z = sbuf.tile([BATCH, OUT], F32)
-        minus_zx = sbuf.tile([BATCH, OUT], F32)
-        log_part = sbuf.tile([BATCH, OUT], F32)
-        relu_sum_0 = sbuf.tile([BATCH, 1], F32)
-        log_sum = sbuf.tile([BATCH, 1], F32)
-        vector_sums = sbuf.tile([BATCH, 2], F32)
-        for cols in halves:
-            nc.vector.scalar_tensor_tensor(
-                out=abs_th[:, cols], in0=th[:, cols], scalar=-1.0, in1=th[:, cols],
-                op0=ALU.mult, op1=ALU.max,
-            )
-            nc.vector.tensor_scalar(
-                out=sig[:, cols], in0=th[:, cols], scalar1=0.5, scalar2=0.5,
-                op0=ALU.mult, op1=ALU.add,
-            )
+            nc.scalar.activation(out=sig[:, cols], in_=z[:, cols], func=ACT.Sigmoid)
             nc.sync.dma_start(out=out_1[:, cols], in_=sig[:, cols])
-        nc.scalar.activation(
-            out=relu_z[:, halves[0]], in_=z[:, halves[0]], func=ACT.Relu, accum_out=relu_sum_0[:]
-        )
+
+        z_held = sbuf.tile([BATCH, OUT], F32)
+        minus_zx = sbuf.tile([BATCH, OUT], F32)
+        sig_held = sbuf.tile([BATCH, OUT], F32)
+        log_part = sbuf.tile([BATCH, OUT], F32)
+        vector_sums = sbuf.tile([BATCH, 2], F32)
+        log_sum = sbuf.tile([BATCH, 1], F32)
         nc.vector.tensor_scalar(
-            out=relu_z[:, halves[1]], in0=z[:, halves[1]], scalar1=0.0, scalar2=None,
+            out=z_held[:], in0=z[:], scalar1=-CLAMP, scalar2=None,
             op0=ALU.max, op1=ALU.add, accum_out=vector_sums[:, 0:1],
         )
-        nc.scalar.activation(
-            out=log_part[:], in_=abs_th[:], func=ACT.Ln, scale=0.5, bias=half[:],
-            accum_out=log_sum[:],
+        nc.vector.tensor_scalar(
+            out=sig_held[:], in0=sig[:], scalar1=SIGMOID_FLOOR, scalar2=None, op0=ALU.max
         )
+        nc.scalar.activation(out=log_part[:], in_=sig_held[:], func=ACT.Ln, accum_out=log_sum[:])
         nc.vector.scalar_tensor_tensor(
             out=minus_zx[:], in0=z[:], scalar=-1.0, in1=x_sb[:],
             op0=ALU.mult, op1=ALU.mult, accum_out=vector_sums[:, 1:2],
         )
 
-        vector_total = sbuf.tile([BATCH, 1], F32)
-        nc.vector.tensor_tensor(
-            out=vector_total[:], in0=vector_sums[:, 0:1], in1=vector_sums[:, 1:2], op=ALU.add
-        )
-        nc.vector.scalar_tensor_tensor(
-            out=bce_cols[:, 0:1], in0=relu_sum_0[:], scalar=log_sum[:], in1=vector_total[:],
-            op0=ALU.subtract, op1=ALU.add,
+        nc.vector.tensor_scalar(
+            out=bce_cols[:, 0:1], in0=vector_sums[:, 0:1],
+            scalar1=vector_sums[:, 1:2], scalar2=log_sum[:], op0=ALU.add, op1=ALU.subtract,
         )
         bce_rows = sbuf.tile([BATCH, SQUARE], F32, align_bytes=64)
         nc.vector.transpose(out=bce_rows[:], in_=bce_cols[:])

@@ -20,6 +20,7 @@ D2 = 512
 OUT = 1024
 BLOCK = 512
 SHARE = BLOCK // 2
+PART = SHARE // 2
 RUN = 4
 DB2_ROWS = OUT // P
 SQUARE = 32
@@ -29,8 +30,8 @@ SIGMOID_FLOOR = 1.0 / (1.0 + math.exp(CLAMP))
 FLOPS = 2 * BATCH * D1 * D2 + 2 * BATCH * D2 * OUT
 
 
-def regroup(copy, grouped, raw, first):
-    cols = slice(first, first + SHARE)
+def regroup(copy, grouped, raw, first, width):
+    cols = slice(first, first + width)
     copy(
         out=grouped[:, cols, :].rearrange("p (c i) t -> p c t i", i=RUN),
         in_=raw[:, :, cols].rearrange("p t (c i) -> p c t i", i=RUN),
@@ -51,10 +52,11 @@ def tile_vae_pb_s_kernel(tc, h_dec0, x, dw1, db1, dw2, db2, out_0, out_1):
         name="psum", bufs=1
     ) as psum, tc.manual_schedule():
         raw1 = sbuf.tile([P, PACK, D2], BF16)
-        nc.sync.dma_start(
-            out=raw1[:].rearrange("p (u e) c -> p u (e c)", e=PAIR),
-            in_=dw1.rearrange("(u p e) c -> p u (e c)", p=P, e=PAIR),
-        )
+        for first in range(0, D2, SHARE):
+            cols = slice(first, first + SHARE)
+            nc.sync.dma_start(
+                out=raw1[:, :, cols], in_=dw1[:, cols].rearrange("(p t) c -> p t c", t=PACK)
+            )
         a_rows = sbuf.tile([BATCH, D1], BF16)
         nc.sync.dma_start(out=a_rows[:], in_=h_dec0)
         bias_rows = sbuf.tile([P, P], BF16)
@@ -87,15 +89,16 @@ def tile_vae_pb_s_kernel(tc, h_dec0, x, dw1, db1, dw2, db2, out_0, out_1):
         codes1 = sbuf.tile([P, D2], U32, align_bytes=64)
         scales1 = sbuf.tile([P, D2], U8, align_bytes=64)
         values1 = grouped1[:].rearrange("p c t -> p (c t)")
-        regroup(nc.vector.tensor_copy, grouped1, raw1, 0)
-        regroup(nc.scalar.copy, grouped1, raw1, SHARE)
+        regroup(nc.vector.tensor_copy, grouped1, raw1, 0, SHARE)
+        regroup(nc.vector.tensor_copy, grouped1, raw1, SHARE, PART)
+        regroup(nc.scalar.copy, grouped1, raw1, SHARE + PART, PART)
         quantise(nc, codes1, scales1, values1, 0, SHARE)
         quantise(nc, codes1, scales1, values1, SHARE, SHARE)
 
         a_words = a_rows[:].bitcast(F32)
         a_t_ps = psum.tile([P, PAIR, BATCH], F32)
         for u in range(PAIR):
-            nc.tensor.transpose(a_t_ps[:, u, :], a_words[:, u * P : (u + 1) * P], ident_f32[:])
+            nc.tensor.transpose(a_t_ps[:, u, :], a_words[:, u:a_words.shape[1]:PAIR], ident_f32[:])
         a_grouped = sbuf.tile([P, BATCH, PAIR], F32, align_bytes=64)
         nc.scalar.copy(out=a_grouped[:], in_=a_t_ps[:].rearrange("p u b -> p b u"))
         a_codes = sbuf.tile([P, BATCH], U32, align_bytes=64)
@@ -113,7 +116,7 @@ def tile_vae_pb_s_kernel(tc, h_dec0, x, dw1, db1, dw2, db2, out_0, out_1):
         codes2 = sbuf.tile([P, OUT], U32, align_bytes=64)
         scales2 = sbuf.tile([P, OUT], U8, align_bytes=64)
         values2 = grouped2[:].rearrange("p c t -> p (c t)")
-        regroup(nc.scalar.copy, grouped2, raw2, SHARE)
+        regroup(nc.scalar.copy, grouped2, raw2, SHARE + PART, PART)
         h_ps = [psum.tile([P, PAIR, BATCH], F32, name="h_ps%d" % i) for i in range(PACK // PAIR)]
         for t in range(PACK):
             cols = slice(t * P, (t + 1) * P)
@@ -134,6 +137,7 @@ def tile_vae_pb_s_kernel(tc, h_dec0, x, dw1, db1, dw2, db2, out_0, out_1):
             )
         h_grouped = sbuf.tile([P, BATCH, PACK], BF16, align_bytes=64)
         nc.scalar.copy(out=h_grouped[:], in_=h_planes[:].rearrange("p t b -> p b t"))
+        regroup(nc.scalar.copy, grouped2, raw2, BLOCK + SHARE + PART, PART)
         h_codes = sbuf.tile([P, BATCH], U32, align_bytes=64)
         h_scales = sbuf.tile([P, BATCH], U8, align_bytes=64)
 
@@ -148,14 +152,15 @@ def tile_vae_pb_s_kernel(tc, h_dec0, x, dw1, db1, dw2, db2, out_0, out_1):
         warm_sigmoid = sbuf.tile([P, 1], F32)
         nc.scalar.activation(out=warm_sigmoid[:], in_=half[:], func=ACT.Sigmoid)
 
-        regroup(nc.vector.tensor_copy, grouped2, raw2, 0)
-        regroup(nc.vector.tensor_copy, grouped2, raw2, BLOCK)
+        regroup(nc.vector.tensor_copy, grouped2, raw2, 0, SHARE)
+        regroup(nc.vector.tensor_copy, grouped2, raw2, SHARE, PART)
         quantise(nc, codes2, scales2, values2, 0, SHARE)
-        regroup(nc.vector.tensor_copy, grouped2, raw2, BLOCK + SHARE)
+        regroup(nc.vector.tensor_copy, grouped2, raw2, BLOCK, SHARE)
         quantise(nc, codes2, scales2, values2, SHARE, SHARE)
+        regroup(nc.vector.tensor_copy, grouped2, raw2, BLOCK + SHARE, PART)
         quantise(nc, codes2, scales2, values2, BLOCK, SHARE)
-        quantise(nc, codes2, scales2, values2, BLOCK + SHARE, SHARE)
         quantise(nc, h_codes, h_scales, h_grouped[:].rearrange("p b t -> p (b t)"), 0, BATCH)
+        quantise(nc, codes2, scales2, values2, BLOCK + SHARE, SHARE)
         nc.vector.tensor_copy(out=db2_all[:], in_=db2_ps[:])
 
         halves = [slice(first, first + BLOCK) for first in range(0, OUT, BLOCK)]

@@ -96,7 +96,7 @@ def tile_vae_pb_s_kernel(tc, h_dec0, x, dw1, db1, dw2, db2, out_0, out_1):
         quantise(nc, codes1, scales1, values1, SHARE, SHARE)
 
         a_words = a_rows[:].bitcast(F32)
-        a_t_ps = psum.tile([P, PAIR, BATCH], F32)
+        a_t_ps = psum.tile([P, PAIR, BATCH], F32, name="bank0")
         for u in range(PAIR):
             nc.tensor.transpose(a_t_ps[:, u, :], a_words[:, u:a_words.shape[1]:PAIR], ident_f32[:])
         a_grouped = sbuf.tile([P, BATCH, PAIR], F32, align_bytes=64)
@@ -163,11 +163,11 @@ def tile_vae_pb_s_kernel(tc, h_dec0, x, dw1, db1, dw2, db2, out_0, out_1):
         quantise(nc, codes2, scales2, values2, BLOCK + SHARE, SHARE)
         nc.vector.tensor_copy(out=db2_all[:], in_=db2_ps[:])
 
-        halves = [slice(first, first + BLOCK) for first in range(0, OUT, BLOCK)]
         z = sbuf.tile([BATCH, OUT], F32)
         sig = sbuf.tile([BATCH, OUT], F32)
-        for b, cols in enumerate(halves):
-            logits_ps = psum.tile([BATCH, BLOCK], F32, name="logits_ps%d" % b)
+        for b in range(OUT // SHARE):
+            cols = slice(b * SHARE, (b + 1) * SHARE)
+            logits_ps = psum.tile([BATCH, SHARE], F32, name="bank%d" % b)
             nc.tensor.matmul_mx(
                 out=logits_ps[:],
                 lhsT=h_codes[:].bitcast(FP8X4),
@@ -181,30 +181,28 @@ def tile_vae_pb_s_kernel(tc, h_dec0, x, dw1, db1, dw2, db2, out_0, out_1):
                 out=z[:, cols], in0=logits_ps[:], in1=db2_all[:, cols], op=ALU.add
             )
             nc.scalar.activation(out=sig[:, cols], in_=z[:, cols], func=ACT.Sigmoid)
-            nc.sync.dma_start(out=out_1[:, cols], in_=sig[:, cols])
+            if b % 2 == 1:
+                stored = slice((b - 1) * SHARE, (b + 1) * SHARE)
+                nc.sync.dma_start(out=out_1[:, stored], in_=sig[:, stored])
 
-        z_held = sbuf.tile([BATCH, OUT], F32)
-        minus_zx = sbuf.tile([BATCH, OUT], F32)
+        linear = sbuf.tile([BATCH, OUT], F32)
+        zx = sbuf.tile([BATCH, OUT], F32)
         sig_held = sbuf.tile([BATCH, OUT], F32)
         log_part = sbuf.tile([BATCH, OUT], F32)
-        vector_sums = sbuf.tile([BATCH, 2], F32)
+        linear_sum = sbuf.tile([BATCH, 1], F32)
         log_sum = sbuf.tile([BATCH, 1], F32)
-        nc.vector.tensor_scalar(
-            out=z_held[:], in0=z[:], scalar1=-CLAMP, scalar2=None,
-            op0=ALU.max, op1=ALU.add, accum_out=vector_sums[:, 0:1],
-        )
+        nc.vector.tensor_tensor(out=zx[:], in0=z[:], in1=x_sb[:], op=ALU.mult)
         nc.vector.tensor_scalar(
             out=sig_held[:], in0=sig[:], scalar1=SIGMOID_FLOOR, scalar2=None, op0=ALU.max
         )
         nc.scalar.activation(out=log_part[:], in_=sig_held[:], func=ACT.Ln, accum_out=log_sum[:])
         nc.vector.scalar_tensor_tensor(
-            out=minus_zx[:], in0=z[:], scalar=-1.0, in1=x_sb[:],
-            op0=ALU.mult, op1=ALU.mult, accum_out=vector_sums[:, 1:2],
+            out=linear[:], in0=z[:], scalar=-CLAMP, in1=zx[:],
+            op0=ALU.max, op1=ALU.subtract, accum_out=linear_sum[:],
         )
 
         nc.vector.tensor_scalar(
-            out=bce_cols[:, 0:1], in0=vector_sums[:, 0:1],
-            scalar1=vector_sums[:, 1:2], scalar2=log_sum[:], op0=ALU.add, op1=ALU.subtract,
+            out=bce_cols[:, 0:1], in0=linear_sum[:], scalar1=log_sum[:], scalar2=None, op0=ALU.subtract
         )
         bce_rows = sbuf.tile([BATCH, SQUARE], F32, align_bytes=64)
         nc.vector.transpose(out=bce_rows[:], in_=bce_cols[:])

@@ -21,6 +21,7 @@ OUT = 1024
 BLOCK = 512
 SHARE = BLOCK // 2
 PART = SHARE // 2
+SCALAR_FIRST = 192
 RUN = 4
 DB2_ROWS = OUT // P
 SQUARE = 32
@@ -30,11 +31,13 @@ SIGMOID_FLOOR = 1.0 / (1.0 + math.exp(CLAMP))
 FLOPS = 2 * BATCH * D1 * D2 + 2 * BATCH * D2 * OUT
 
 
-def regroup(copy, grouped, raw, first, width):
-    cols = slice(first, first + width)
+def regroup(copy, grouped, chunks, first, width):
+    chunk_width = chunks[0].shape[2]
+    raw = chunks[first // chunk_width]
+    start = first % chunk_width
     copy(
-        out=grouped[:, cols, :].rearrange("p (c i) t -> p c t i", i=RUN),
-        in_=raw[:, :, cols].rearrange("p t (c i) -> p c t i", i=RUN),
+        out=grouped[:, first : first + width, :].rearrange("p (c i) t -> p c t i", i=RUN),
+        in_=raw[:, :, start : start + width].rearrange("p t (c i) -> p c t i", i=RUN),
     )
 
 
@@ -51,26 +54,22 @@ def tile_vae_pb_s_kernel(tc, h_dec0, x, dw1, db1, dw2, db2, out_0, out_1):
     with tc.tile_pool(name="sbuf", bufs=1) as sbuf, tc.psum_pool(
         name="psum", bufs=1
     ) as psum, tc.manual_schedule():
-        raw1 = sbuf.tile([P, PACK, D2], BF16)
-        for first in range(0, D2, SHARE):
-            cols = slice(first, first + SHARE)
-            nc.sync.dma_start(
-                out=raw1[:, :, cols], in_=dw1[:, cols].rearrange("(p t) c -> p t c", t=PACK)
-            )
-        a_rows = sbuf.tile([BATCH, D1], BF16)
-        nc.sync.dma_start(out=a_rows[:], in_=h_dec0)
         bias_rows = sbuf.tile([P, P], BF16)
-        nc.vector.memset(bias_rows[:], 0.0)
+        nc.gpsimd.memset(bias_rows[:], 0.0)
+        raw1 = [sbuf.tile([P, PACK, SHARE], BF16, name="raw1_%d" % i) for i in range(D2 // SHARE)]
+        a_rows = sbuf.tile([BATCH, D1], BF16)
+        dw1_rows = dw1.rearrange("(p t) c -> p t c", t=PACK)
+        nc.sync.dma_start(out=a_rows[:], in_=h_dec0)
+        nc.sync.dma_start(out=raw1[0][:], in_=dw1_rows[:, :, 0:SHARE])
+        nc.sync.dma_start(out=raw1[1][:], in_=dw1_rows[:, :, SHARE:D2])
         nc.sync.dma_start(out=bias_rows[0:DB2_ROWS, :], in_=db2.rearrange("(c n) -> c n", n=P))
         nc.sync.dma_start(
             out=bias_rows[DB2_ROWS : DB2_ROWS + PACK, :], in_=db1.rearrange("(c n) -> c n", n=P)
         )
-        raw2 = sbuf.tile([P, PACK, OUT], BF16)
-        for first in range(0, OUT, BLOCK):
-            cols = slice(first, first + BLOCK)
-            nc.sync.dma_start(
-                out=raw2[:, :, cols], in_=dw2[:, cols].rearrange("(t p) c -> p t c", p=P)
-            )
+        raw2 = [sbuf.tile([P, PACK, BLOCK], BF16, name="raw2_%d" % i) for i in range(OUT // BLOCK)]
+        for i, chunk in enumerate(raw2):
+            cols = slice(i * BLOCK, (i + 1) * BLOCK)
+            nc.sync.dma_start(out=chunk[:], in_=dw2[:, cols].rearrange("(t p) c -> p t c", p=P))
         x_sb = sbuf.tile([BATCH, OUT], BF16)
         nc.sync.dma_start(out=x_sb[:], in_=x)
 
@@ -85,38 +84,38 @@ def tile_vae_pb_s_kernel(tc, h_dec0, x, dw1, db1, dw2, db2, out_0, out_1):
         warm = sbuf.tile([P, 1], F32)
         nc.scalar.activation(out=warm[:], in_=half[:], func=ACT.Silu)
 
-        grouped1 = sbuf.tile([P, D2, PACK], BF16, align_bytes=64)
-        codes1 = sbuf.tile([P, D2], U32, align_bytes=64)
-        scales1 = sbuf.tile([P, D2], U8, align_bytes=64)
-        values1 = grouped1[:].rearrange("p c t -> p (c t)")
-        regroup(nc.vector.tensor_copy, grouped1, raw1, 0, SHARE)
-        regroup(nc.vector.tensor_copy, grouped1, raw1, SHARE, PART)
-        regroup(nc.scalar.copy, grouped1, raw1, SHARE + PART, PART)
-        quantise(nc, codes1, scales1, values1, 0, SHARE)
-        quantise(nc, codes1, scales1, values1, SHARE, SHARE)
-
         a_words = a_rows[:].bitcast(F32)
         a_t_ps = psum.tile([P, PAIR, BATCH], F32, name="bank0")
         for u in range(PAIR):
-            nc.tensor.transpose(a_t_ps[:, u, :], a_words[:, u:a_words.shape[1]:PAIR], ident_f32[:])
+            nc.tensor.transpose(a_t_ps[:, u, :], a_words[:, u : D1 // PAIR : PAIR], ident_f32[:])
         a_grouped = sbuf.tile([P, BATCH, PAIR], F32, align_bytes=64)
-        nc.scalar.copy(out=a_grouped[:], in_=a_t_ps[:].rearrange("p u b -> p b u"))
         a_codes = sbuf.tile([P, BATCH], U32, align_bytes=64)
         a_scales = sbuf.tile([P, BATCH], U8, align_bytes=64)
-        quantise(
-            nc, a_codes, a_scales, a_grouped[:].rearrange("p b u -> p (b u)").bitcast(BF16), 0, BATCH
-        )
 
         bias_t_ps = psum.tile([P, P], BF16)
         nc.tensor.transpose(bias_t_ps[:], bias_rows[:], ident_bf[:])
         bias_cols = sbuf.tile([P, DB2_ROWS + PACK], BF16)
+
+        grouped1 = sbuf.tile([P, D2, PACK], BF16, align_bytes=64)
+        codes1 = sbuf.tile([P, D2], U32, align_bytes=64)
+        scales1 = sbuf.tile([P, D2], U8, align_bytes=64)
+        values1 = grouped1[:].rearrange("p c t -> p (c t)")
+        regroup(nc.scalar.copy, grouped1, raw1, PART, PART)
+        nc.scalar.copy(out=a_grouped[:], in_=a_t_ps[:].rearrange("p u b -> p b u"))
         nc.scalar.copy(out=bias_cols[:], in_=bias_t_ps[:, 0 : DB2_ROWS + PACK])
+        regroup(nc.vector.tensor_copy, grouped1, raw1, 0, PART)
+        regroup(nc.vector.tensor_copy, grouped1, raw1, SHARE, SHARE)
+        quantise(nc, codes1, scales1, values1, 0, SHARE)
+        quantise(
+            nc, a_codes, a_scales, a_grouped[:].rearrange("p b u -> p (b u)").bitcast(BF16), 0, BATCH
+        )
+        quantise(nc, codes1, scales1, values1, SHARE, SHARE)
 
         grouped2 = sbuf.tile([P, OUT, PACK], BF16, align_bytes=64)
         codes2 = sbuf.tile([P, OUT], U32, align_bytes=64)
         scales2 = sbuf.tile([P, OUT], U8, align_bytes=64)
         values2 = grouped2[:].rearrange("p c t -> p (c t)")
-        regroup(nc.scalar.copy, grouped2, raw2, SHARE + PART, PART)
+        regroup(nc.scalar.copy, grouped2, raw2, BLOCK - SCALAR_FIRST, SCALAR_FIRST)
         h_ps = [psum.tile([P, PAIR, BATCH], F32, name="h_ps%d" % i) for i in range(PACK // PAIR)]
         for t in range(PACK):
             cols = slice(t * P, (t + 1) * P)
@@ -129,6 +128,15 @@ def tile_vae_pb_s_kernel(tc, h_dec0, x, dw1, db1, dw2, db2, out_0, out_1):
                 start=True,
                 stop=True,
             )
+        db2_ps = psum.tile([P, OUT], BF16)
+        for c in range(DB2_ROWS):
+            nc.tensor.transpose(
+                db2_ps[:, c * P : (c + 1) * P],
+                bias_cols[:, c : c + 1].to_broadcast([P, P]),
+                ident_bf[:],
+            )
+        db2_all = sbuf.tile([P, OUT], BF16)
+
         h_planes = sbuf.tile([P, PACK, BATCH], BF16)
         for t in range(PACK):
             nc.scalar.activation(
@@ -141,19 +149,11 @@ def tile_vae_pb_s_kernel(tc, h_dec0, x, dw1, db1, dw2, db2, out_0, out_1):
         h_codes = sbuf.tile([P, BATCH], U32, align_bytes=64)
         h_scales = sbuf.tile([P, BATCH], U8, align_bytes=64)
 
-        db2_ps = psum.tile([P, OUT], BF16)
-        for c in range(DB2_ROWS):
-            nc.tensor.transpose(
-                db2_ps[:, c * P : (c + 1) * P],
-                bias_cols[:, c : c + 1].to_broadcast([P, P]),
-                ident_bf[:],
-            )
-        db2_all = sbuf.tile([P, OUT], BF16)
         warm_sigmoid = sbuf.tile([P, 1], F32)
         nc.scalar.activation(out=warm_sigmoid[:], in_=half[:], func=ACT.Sigmoid)
 
         regroup(nc.vector.tensor_copy, grouped2, raw2, 0, SHARE)
-        regroup(nc.vector.tensor_copy, grouped2, raw2, SHARE, PART)
+        regroup(nc.vector.tensor_copy, grouped2, raw2, SHARE, SHARE - SCALAR_FIRST)
         quantise(nc, codes2, scales2, values2, 0, SHARE)
         regroup(nc.vector.tensor_copy, grouped2, raw2, BLOCK, SHARE)
         quantise(nc, codes2, scales2, values2, SHARE, SHARE)

@@ -144,7 +144,7 @@ def tile_vae_pb_s_kernel(tc, h_dec0, x, dw1, db1, dw2, db2, out_0, out_1):
                 bias=bias_cols[:, DB2_ROWS + t : DB2_ROWS + t + 1],
             )
         h_grouped = sbuf.tile([P, BATCH, PACK], BF16, align_bytes=64)
-        nc.scalar.copy(out=h_grouped[:], in_=h_planes[:].rearrange("p t b -> p b t"))
+        regroup(nc.scalar.copy, h_grouped, [h_planes], 0, BATCH)
         regroup(nc.scalar.copy, grouped2, raw2, BLOCK + SHARE + PART, PART)
         h_codes = sbuf.tile([P, BATCH], U32, align_bytes=64)
         h_scales = sbuf.tile([P, BATCH], U8, align_bytes=64)
@@ -191,7 +191,9 @@ def tile_vae_pb_s_kernel(tc, h_dec0, x, dw1, db1, dw2, db2, out_0, out_1):
         log_part = sbuf.tile([BATCH, OUT], F32)
         linear_sum = sbuf.tile([BATCH, 1], F32)
         log_sum = sbuf.tile([BATCH, 1], F32)
-        nc.vector.tensor_tensor(out=zx[:], in0=z[:], in1=x_sb[:], op=ALU.mult)
+        for first in range(0, OUT, BLOCK):
+            cols = slice(first, first + BLOCK)
+            nc.vector.tensor_tensor(out=zx[:, cols], in0=z[:, cols], in1=x_sb[:, cols], op=ALU.mult)
         nc.vector.tensor_scalar(
             out=sig_held[:], in0=sig[:], scalar1=SIGMOID_FLOOR, scalar2=None, op0=ALU.max
         )

@@ -185,19 +185,30 @@ def tile_vae_pb_s_kernel(tc, h_dec0, x, dw1, db1, dw2, db2, out_0, out_1):
                 stored = slice((b - 1) * SHARE, (b + 1) * SHARE)
                 nc.sync.dma_start(out=out_1[:, stored], in_=sig[:, stored])
 
+        quarter = [slice(first, first + SHARE) for first in range(0, OUT, SHARE)]
         linear = sbuf.tile([BATCH, OUT], F32)
         zx = sbuf.tile([BATCH, OUT], F32)
-        sig_held = sbuf.tile([BATCH, OUT], F32)
-        log_part = sbuf.tile([BATCH, OUT], F32)
+        held_1 = sbuf.tile([BATCH, SHARE], F32)
+        log_in = sbuf.tile([BATCH, OUT - SHARE], F32)
+        log_part = sbuf.tile([BATCH, OUT - SHARE], F32)
         linear_sum = sbuf.tile([BATCH, 1], F32)
         log_sum = sbuf.tile([BATCH, 1], F32)
-        for first in range(0, OUT, BLOCK):
-            cols = slice(first, first + BLOCK)
-            nc.vector.tensor_tensor(out=zx[:, cols], in0=z[:, cols], in1=x_sb[:, cols], op=ALU.mult)
+        for cols in quarter[:2]:
+            nc.gpsimd.tensor_tensor(out=zx[:, cols], in0=z[:, cols], in1=x_sb[:, cols], op=ALU.mult)
         nc.vector.tensor_scalar(
-            out=sig_held[:], in0=sig[:], scalar1=SIGMOID_FLOOR, scalar2=None, op0=ALU.max
+            out=held_1[:], in0=sig[:, quarter[1]], scalar1=SIGMOID_FLOOR, scalar2=None, op0=ALU.max
         )
-        nc.scalar.activation(out=log_part[:], in_=sig_held[:], func=ACT.Ln, accum_out=log_sum[:])
+        nc.vector.tensor_tensor(
+            out=zx[:, BLOCK:OUT], in0=z[:, BLOCK:OUT], in1=x_sb[:, BLOCK:OUT], op=ALU.mult
+        )
+        nc.vector.scalar_tensor_tensor(
+            out=log_in[:, 0:SHARE], in0=sig[:, quarter[0]], scalar=SIGMOID_FLOOR, in1=held_1[:],
+            op0=ALU.max, op1=ALU.mult,
+        )
+        nc.vector.tensor_scalar(
+            out=log_in[:, SHARE:], in0=sig[:, BLOCK:OUT], scalar1=SIGMOID_FLOOR, scalar2=None, op0=ALU.max
+        )
+        nc.scalar.activation(out=log_part[:], in_=log_in[:], func=ACT.Ln, accum_out=log_sum[:])
         nc.vector.scalar_tensor_tensor(
             out=linear[:], in0=z[:], scalar=-CLAMP, in1=zx[:],
             op0=ALU.max, op1=ALU.subtract, accum_out=linear_sum[:],

@@ -21,6 +21,7 @@ OUT = 1024
 BLOCK = 512
 SHARE = BLOCK // 2
 PART = SHARE // 2
+BIT = SHARE // 4
 SCALAR_FIRST = 192
 RUN = 4
 DB2_ROWS = OUT // P
@@ -102,9 +103,10 @@ def tile_vae_pb_s_kernel(tc, h_dec0, x, dw1, db1, dw2, db2, out_0, out_1):
         values1 = grouped1[:].rearrange("p c t -> p (c t)")
         regroup(nc.scalar.copy, grouped1, raw1, PART, PART)
         nc.scalar.copy(out=a_grouped[:], in_=a_t_ps[:].rearrange("p u b -> p b u"))
+        regroup(nc.scalar.copy, grouped1, raw1, D2 - BIT, BIT)
         nc.scalar.copy(out=bias_cols[:], in_=bias_t_ps[:, 0 : DB2_ROWS + PACK])
         regroup(nc.vector.tensor_copy, grouped1, raw1, 0, PART)
-        regroup(nc.vector.tensor_copy, grouped1, raw1, SHARE, SHARE)
+        regroup(nc.vector.tensor_copy, grouped1, raw1, SHARE, SHARE - BIT)
         quantise(nc, codes1, scales1, values1, 0, SHARE)
         quantise(
             nc, a_codes, a_scales, a_grouped[:].rearrange("p b u -> p (b u)").bitcast(BF16), 0, BATCH
@@ -145,7 +147,8 @@ def tile_vae_pb_s_kernel(tc, h_dec0, x, dw1, db1, dw2, db2, out_0, out_1):
             )
         h_grouped = sbuf.tile([P, BATCH, PACK], BF16, align_bytes=64)
         regroup(nc.scalar.copy, h_grouped, [h_planes], 0, BATCH)
-        regroup(nc.scalar.copy, grouped2, raw2, BLOCK + SHARE + PART, PART)
+        regroup(nc.scalar.copy, grouped2, raw2, OUT - BIT, BIT)
+        nc.scalar.copy(out=db2_all[:, BLOCK:OUT], in_=db2_ps[:, BLOCK:OUT])
         h_codes = sbuf.tile([P, BATCH], U32, align_bytes=64)
         h_scales = sbuf.tile([P, BATCH], U8, align_bytes=64)
 
@@ -157,11 +160,11 @@ def tile_vae_pb_s_kernel(tc, h_dec0, x, dw1, db1, dw2, db2, out_0, out_1):
         quantise(nc, codes2, scales2, values2, 0, SHARE)
         regroup(nc.vector.tensor_copy, grouped2, raw2, BLOCK, SHARE)
         quantise(nc, codes2, scales2, values2, SHARE, SHARE)
-        regroup(nc.vector.tensor_copy, grouped2, raw2, BLOCK + SHARE, PART)
+        regroup(nc.vector.tensor_copy, grouped2, raw2, BLOCK + SHARE, SHARE - BIT)
         quantise(nc, codes2, scales2, values2, BLOCK, SHARE)
         quantise(nc, h_codes, h_scales, h_grouped[:].rearrange("p b t -> p (b t)"), 0, BATCH)
         quantise(nc, codes2, scales2, values2, BLOCK + SHARE, SHARE)
-        nc.vector.tensor_copy(out=db2_all[:], in_=db2_ps[:])
+        nc.vector.tensor_copy(out=db2_all[:, 0:BLOCK], in_=db2_ps[:, 0:BLOCK])
 
         z = sbuf.tile([BATCH, OUT], F32)
         sig = sbuf.tile([BATCH, OUT], F32)

@@ -22,7 +22,6 @@ BLOCK = 512
 SHARE = BLOCK // 2
 PART = SHARE // 2
 BIT = SHARE // 4
-SCALAR_FIRST = 192
 RUN = 4
 DB2_ROWS = OUT // P
 SQUARE = 32
@@ -67,9 +66,9 @@ def tile_vae_pb_s_kernel(tc, h_dec0, x, dw1, db1, dw2, db2, out_0, out_1):
         nc.sync.dma_start(
             out=bias_rows[DB2_ROWS : DB2_ROWS + PACK, :], in_=db1.rearrange("(c n) -> c n", n=P)
         )
-        raw2 = [sbuf.tile([P, PACK, BLOCK], BF16, name="raw2_%d" % i) for i in range(OUT // BLOCK)]
+        raw2 = [sbuf.tile([P, PACK, SHARE], BF16, name="raw2_%d" % i) for i in range(OUT // SHARE)]
         for i, chunk in enumerate(raw2):
-            cols = slice(i * BLOCK, (i + 1) * BLOCK)
+            cols = slice(i * SHARE, (i + 1) * SHARE)
             nc.sync.dma_start(out=chunk[:], in_=dw2[:, cols].rearrange("(t p) c -> p t c", p=P))
         x_sb = sbuf.tile([BATCH, OUT], BF16)
         nc.sync.dma_start(out=x_sb[:], in_=x)
@@ -117,7 +116,7 @@ def tile_vae_pb_s_kernel(tc, h_dec0, x, dw1, db1, dw2, db2, out_0, out_1):
         codes2 = sbuf.tile([P, OUT], U32, align_bytes=64)
         scales2 = sbuf.tile([P, OUT], U8, align_bytes=64)
         values2 = grouped2[:].rearrange("p c t -> p (c t)")
-        regroup(nc.scalar.copy, grouped2, raw2, BLOCK - SCALAR_FIRST, SCALAR_FIRST)
+        regroup(nc.scalar.copy, grouped2, raw2, 0, SHARE)
         h_ps = [psum.tile([P, PAIR, BATCH], F32, name="h_ps%d" % i) for i in range(PACK // PAIR)]
         for t in range(PACK):
             cols = slice(t * P, (t + 1) * P)
@@ -155,16 +154,15 @@ def tile_vae_pb_s_kernel(tc, h_dec0, x, dw1, db1, dw2, db2, out_0, out_1):
         warm_sigmoid = sbuf.tile([P, 1], F32)
         nc.scalar.activation(out=warm_sigmoid[:], in_=half[:], func=ACT.Sigmoid)
 
-        regroup(nc.vector.tensor_copy, grouped2, raw2, 0, SHARE)
-        regroup(nc.vector.tensor_copy, grouped2, raw2, SHARE, SHARE - SCALAR_FIRST)
-        quantise(nc, codes2, scales2, values2, 0, SHARE)
+        regroup(nc.vector.tensor_copy, grouped2, raw2, SHARE, SHARE)
         regroup(nc.vector.tensor_copy, grouped2, raw2, BLOCK, SHARE)
+        quantise(nc, codes2, scales2, values2, 0, SHARE)
         quantise(nc, codes2, scales2, values2, SHARE, SHARE)
         regroup(nc.vector.tensor_copy, grouped2, raw2, BLOCK + SHARE, SHARE - BIT)
         quantise(nc, codes2, scales2, values2, BLOCK, SHARE)
         quantise(nc, h_codes, h_scales, h_grouped[:].rearrange("p b t -> p (b t)"), 0, BATCH)
-        quantise(nc, codes2, scales2, values2, BLOCK + SHARE, SHARE)
         nc.vector.tensor_copy(out=db2_all[:, 0:BLOCK], in_=db2_ps[:, 0:BLOCK])
+        quantise(nc, codes2, scales2, values2, BLOCK + SHARE, SHARE)
 
         z = sbuf.tile([BATCH, OUT], F32)
         sig = sbuf.tile([BATCH, OUT], F32)

import math

import concourse.mybir as mybir
from concourse.masks import make_identity

FP8X4 = mybir.dt.float8_e4m3fn_x4
BF16 = mybir.dt.bfloat16
F32 = mybir.dt.float32
U32 = mybir.dt.uint32
U8 = mybir.dt.uint8
ALU = mybir.AluOpType
ACT = mybir.ActivationFunctionType

P = 128
PACK = 4
PAIR = 2
BATCH = 128
D1 = 512
D2 = 512
OUT = 1024
BLOCK = 512
SHARE = BLOCK // 2
PART = SHARE // 2
BIT = SHARE // 4
RUN = 4
DB2_ROWS = OUT // P
SQUARE = 32
CLAMP = 30.0
SIGMOID_FLOOR = 1.0 / (1.0 + math.exp(CLAMP))

FLOPS = 2 * BATCH * D1 * D2 + 2 * BATCH * D2 * OUT


def regroup(copy, grouped, chunks, first, width):
    chunk_width = chunks[0].shape[2]
    raw = chunks[first // chunk_width]
    start = first % chunk_width
    copy(
        out=grouped[:, first : first + width, :].rearrange("p (c i) t -> p c t i", i=RUN),
        in_=raw[:, :, start : start + width].rearrange("p t (c i) -> p c t i", i=RUN),
    )


def quantise(nc, codes, scales, values, first, width):
    nc.vector.quantize_mx(
        out=codes[:, first : first + width].bitcast(FP8X4),
        scales=scales[:, first : first + width],
        in_=values[:, PACK * first : PACK * (first + width)],
    )


def tile_vae_pb_s_kernel(tc, h_dec0, x, dw1, db1, dw2, db2, out_0, out_1):
    nc = tc.nc
    with tc.tile_pool(name="sbuf", bufs=1) as sbuf, tc.psum_pool(
        name="psum", bufs=1
    ) as psum, tc.manual_schedule():
        bias_rows = sbuf.tile([P, P], BF16)
        nc.gpsimd.memset(bias_rows[:], 0.0)
        raw1 = [sbuf.tile([P, PACK, SHARE], BF16, name="raw1_%d" % i) for i in range(D2 // SHARE)]
        a_rows = sbuf.tile([BATCH, D1], BF16)
        dw1_rows = dw1.rearrange("(p t) c -> p t c", t=PACK)
        nc.sync.dma_start(out=a_rows[:], in_=h_dec0)
        nc.sync.dma_start(out=raw1[0][:], in_=dw1_rows[:, :, 0:SHARE])
        nc.sync.dma_start(out=raw1[1][:], in_=dw1_rows[:, :, SHARE:D2])
        nc.sync.dma_start(out=bias_rows[0:DB2_ROWS, :], in_=db2.rearrange("(c n) -> c n", n=P))
        nc.sync.dma_start(
            out=bias_rows[DB2_ROWS : DB2_ROWS + PACK, :], in_=db1.rearrange("(c n) -> c n", n=P)
        )
        raw2 = [sbuf.tile([P, PACK, SHARE], BF16, name="raw2_%d" % i) for i in range(OUT // SHARE)]
        for i, chunk in enumerate(raw2):
            cols = slice(i * SHARE, (i + 1) * SHARE)
            nc.sync.dma_start(out=chunk[:], in_=dw2[:, cols].rearrange("(t p) c -> p t c", p=P))
        x_sb = sbuf.tile([BATCH, OUT], BF16)
        nc.sync.dma_start(out=x_sb[:], in_=x)

        ident_f32 = sbuf.tile([P, P], F32)
        make_identity(nc, ident_f32[:])
        ident_bf = sbuf.tile([P, P], BF16)
        make_identity(nc, ident_bf[:])
        half = sbuf.tile([P, 1], F32)
        nc.vector.memset(half[:], 0.5)
        bce_cols = sbuf.tile([BATCH, SQUARE], F32, align_bytes=64)
        nc.vector.memset(bce_cols[:], 0.0)
        warm = sbuf.tile([P, 1], F32)
        nc.scalar.activation(out=warm[:], in_=half[:], func=ACT.Silu)

        a_words = a_rows[:].bitcast(F32)
        a_t_ps = psum.tile([P, PAIR, BATCH], F32, name="bank0")
        for u in range(PAIR):
            nc.tensor.transpose(a_t_ps[:, u, :], a_words[:, u : D1 // PAIR : PAIR], ident_f32[:])
        a_grouped = sbuf.tile([P, BATCH, PAIR], F32, align_bytes=64)
        a_codes = sbuf.tile([P, BATCH], U32, align_bytes=64)
        a_scales = sbuf.tile([P, BATCH], U8, align_bytes=64)

        bias_t_ps = psum.tile([P, P], BF16)
        nc.tensor.transpose(bias_t_ps[:], bias_rows[:], ident_bf[:])
        bias_cols = sbuf.tile([P, DB2_ROWS + PACK], BF16)

        grouped1 = sbuf.tile([P, D2, PACK], BF16, align_bytes=64)
        codes1 = sbuf.tile([P, D2], U32, align_bytes=64)
        scales1 = sbuf.tile([P, D2], U8, align_bytes=64)
        values1 = grouped1[:].rearrange("p c t -> p (c t)")
        regroup(nc.scalar.copy, grouped1, raw1, PART, PART)
        nc.scalar.copy(out=a_grouped[:], in_=a_t_ps[:].rearrange("p u b -> p b u"))
        regroup(nc.scalar.copy, grouped1, raw1, D2 - BIT, BIT)
        nc.scalar.copy(out=bias_cols[:], in_=bias_t_ps[:, 0 : DB2_ROWS + PACK])
        regroup(nc.vector.tensor_copy, grouped1, raw1, 0, PART)
        regroup(nc.vector.tensor_copy, grouped1, raw1, SHARE, SHARE - BIT)
        quantise(nc, codes1, scales1, values1, 0, SHARE)
        quantise(
            nc, a_codes, a_scales, a_grouped[:].rearrange("p b u -> p (b u)").bitcast(BF16), 0, BATCH
        )
        quantise(nc, codes1, scales1, values1, SHARE, SHARE)

        grouped2 = sbuf.tile([P, OUT, PACK], BF16, align_bytes=64)
        codes2 = sbuf.tile([P, OUT], U32, align_bytes=64)
        scales2 = sbuf.tile([P, OUT], U8, align_bytes=64)
        values2 = grouped2[:].rearrange("p c t -> p (c t)")
        regroup(nc.scalar.copy, grouped2, raw2, 0, SHARE)
        h_ps = [psum.tile([P, PAIR, BATCH], F32, name="h_ps%d" % i) for i in range(PACK // PAIR)]
        for t in range(PACK):
            cols = slice(t * P, (t + 1) * P)
            nc.tensor.matmul_mx(
                out=h_ps[t // PAIR][:, t % PAIR, :],
                lhsT=codes1[:, cols].bitcast(FP8X4),
                lhsT_scale=scales1[:, cols],
                rhs=a_codes[:].bitcast(FP8X4),
                rhs_scale=a_scales[:],
                start=True,
                stop=True,
            )
        db2_ps = psum.tile([P, OUT], BF16)
        for c in range(DB2_ROWS):
            nc.tensor.transpose(
                db2_ps[:, c * P : (c + 1) * P],
                bias_cols[:, c : c + 1].to_broadcast([P, P]),
                ident_bf[:],
            )
        db2_all = sbuf.tile([P, OUT], BF16)

        h_planes = sbuf.tile([P, PACK, BATCH], BF16)
        for t in range(PACK):
            nc.scalar.activation(
                out=h_planes[:, t, :], in_=h_ps[t // PAIR][:, t % PAIR, :], func=ACT.Silu,
                bias=bias_cols[:, DB2_ROWS + t : DB2_ROWS + t + 1],
            )
        h_grouped = sbuf.tile([P, BATCH, PACK], BF16, align_bytes=64)
        regroup(nc.scalar.copy, h_grouped, [h_planes], 0, BATCH)
        regroup(nc.scalar.copy, grouped2, raw2, OUT - BIT, BIT)
        nc.scalar.copy(out=db2_all[:, BLOCK:OUT], in_=db2_ps[:, BLOCK:OUT])
        h_codes = sbuf.tile([P, BATCH], U32, align_bytes=64)
        h_scales = sbuf.tile([P, BATCH], U8, align_bytes=64)

        warm_sigmoid = sbuf.tile([P, 1], F32)
        nc.scalar.activation(out=warm_sigmoid[:], in_=half[:], func=ACT.Sigmoid)

        regroup(nc.vector.tensor_copy, grouped2, raw2, SHARE, SHARE)
        regroup(nc.vector.tensor_copy, grouped2, raw2, BLOCK, SHARE)
        quantise(nc, codes2, scales2, values2, 0, SHARE)
        quantise(nc, codes2, scales2, values2, SHARE, SHARE)
        regroup(nc.vector.tensor_copy, grouped2, raw2, BLOCK + SHARE, SHARE - BIT)
        quantise(nc, codes2, scales2, values2, BLOCK, SHARE)
        quantise(nc, h_codes, h_scales, h_grouped[:].rearrange("p b t -> p (b t)"), 0, BATCH)
        nc.vector.tensor_copy(out=db2_all[:, 0:BLOCK], in_=db2_ps[:, 0:BLOCK])
        quantise(nc, codes2, scales2, values2, BLOCK + SHARE, SHARE)

        z = sbuf.tile([BATCH, OUT], F32)
        sig = sbuf.tile([BATCH, OUT], F32)
        for b in range(OUT // SHARE):
            cols = slice(b * SHARE, (b + 1) * SHARE)
            logits_ps = psum.tile([BATCH, SHARE], F32, name="bank%d" % b)
            nc.tensor.matmul_mx(
                out=logits_ps[:],
                lhsT=h_codes[:].bitcast(FP8X4),
                lhsT_scale=h_scales[:],
                rhs=codes2[:, cols].bitcast(FP8X4),
                rhs_scale=scales2[:, cols],
                start=True,
                stop=True,
            )
            nc.vector.tensor_tensor(
                out=z[:, cols], in0=logits_ps[:], in1=db2_all[:, cols], op=ALU.add
            )
            nc.scalar.activation(out=sig[:, cols], in_=z[:, cols], func=ACT.Sigmoid)
            if b % 2 == 1:
                stored = slice((b - 1) * SHARE, (b + 1) * SHARE)
                nc.sync.dma_start(out=out_1[:, stored], in_=sig[:, stored])

        quarter = [slice(first, first + SHARE) for first in range(0, OUT, SHARE)]
        linear = sbuf.tile([BATCH, OUT], F32)
        zx = sbuf.tile([BATCH, OUT], F32)
        held_1 = sbuf.tile([BATCH, SHARE], F32)
        log_in = sbuf.tile([BATCH, OUT - SHARE], F32)
        log_part = sbuf.tile([BATCH, OUT - SHARE], F32)
        linear_sum = sbuf.tile([BATCH, 1], F32)
        log_sum = sbuf.tile([BATCH, 1], F32)
        for cols in quarter[:2]:
            nc.gpsimd.tensor_tensor(out=zx[:, cols], in0=z[:, cols], in1=x_sb[:, cols], op=ALU.mult)
        nc.vector.tensor_scalar(
            out=held_1[:], in0=sig[:, quarter[1]], scalar1=SIGMOID_FLOOR, scalar2=None, op0=ALU.max
        )
        nc.vector.tensor_tensor(
            out=zx[:, BLOCK:OUT], in0=z[:, BLOCK:OUT], in1=x_sb[:, BLOCK:OUT], op=ALU.mult
        )
        nc.vector.scalar_tensor_tensor(
            out=log_in[:, 0:SHARE], in0=sig[:, quarter[0]], scalar=SIGMOID_FLOOR, in1=held_1[:],
            op0=ALU.max, op1=ALU.mult,
        )
        nc.vector.tensor_scalar(
            out=log_in[:, SHARE:], in0=sig[:, BLOCK:OUT], scalar1=SIGMOID_FLOOR, scalar2=None, op0=ALU.max
        )
        nc.scalar.activation(out=log_part[:], in_=log_in[:], func=ACT.Ln, accum_out=log_sum[:])
        nc.vector.scalar_tensor_tensor(
            out=linear[:], in0=z[:], scalar=-CLAMP, in1=zx[:],
            op0=ALU.max, op1=ALU.subtract, accum_out=linear_sum[:],
        )

        nc.vector.tensor_scalar(
            out=bce_cols[:, 0:1], in0=linear_sum[:], scalar1=log_sum[:], scalar2=None, op0=ALU.subtract
        )
        bce_rows = sbuf.tile([BATCH, SQUARE], F32, align_bytes=64)
        nc.vector.transpose(out=bce_rows[:], in_=bce_cols[:])
        nc.sync.dma_start(
            out=out_0.rearrange("(q j) -> q j", j=SQUARE), in_=bce_rows[0:BATCH:SQUARE, :]
        )
